import numpy as np
import ml_dtypes


def mxq(x, axis, fmt="e4m3"):
    dtype, down = {"e4m3": (ml_dtypes.float8_e4m3fn, 7), "e5m2": (ml_dtypes.float8_e5m2, 14)}[fmt]
    v = np.moveaxis(np.asarray(x, np.float32).astype(ml_dtypes.bfloat16).astype(np.float64), axis, -1)
    blocks = v.reshape(v.shape[:-1] + (-1, 32))
    amax = np.abs(blocks).max(-1, keepdims=True)
    byte = np.maximum(np.where(amax > 0, np.frexp(amax)[1] - 1 + 127, 0) - down, 1)
    scale = np.exp2(byte - 127.0)
    codes = (blocks / scale).astype(np.float32).astype(dtype).astype(np.float64)
    return np.moveaxis((codes * scale).reshape(v.shape), -1, axis)


WIDE = False


def mx_kscale(k):
    if not WIDE:
        return np.ones(k)
    levels = np.array([10, -10, 5, -5, 0])
    if k % 512:
        return np.exp2(np.random.permutation(np.resize(levels, k // 32))).repeat(32)
    a = np.empty((k // 512, 16))
    for p in range(k // 512):
        a[p, :8] = np.random.permutation(np.resize(levels, 8))
        for g in range(8):
            far = levels[np.abs(levels - a[p, g]) >= 10]
            a[p, g + 8] = far[np.random.randint(len(far))]
    return np.exp2(a.ravel()).repeat(32)


BF16 = ml_dtypes.bfloat16


def bf(x):
    return np.asarray(x, np.float32).astype(BF16)


def f64(x):
    return np.asarray(x).astype(np.float64)


H, D_CONTENT, D_POS, D_K, D_V, B, L = 8, 768, 256, 128, 128, 4, 256
D_MODEL = D_CONTENT + D_POS
T = B * L
DV1 = D_V // 2
KP = H * DV1
EPS = 1e-3


def setup_inputs():
    s1, s2 = mx_kscale(KP), mx_kscale(KP)
    sc = np.concatenate([s1.reshape(H, DV1), s2.reshape(H, DV1)], axis=1)
    return {
        "attn_out": bf(np.random.standard_normal((H, B, L, D_V)) * 0.4 * sc[:, None, None, :]),
        "inp": bf(np.random.standard_normal((T, D_MODEL)) * 0.05 + np.random.standard_normal((T, 1)) * 0.03),
        "w_proj1": bf(np.random.standard_normal((KP, D_CONTENT)) * 0.1 / np.sqrt(KP) / s1[:, None]),
        "w_proj2": bf(np.random.standard_normal((KP, D_POS)) * 0.1 / np.sqrt(KP) / s2[:, None]),
        "ln_a": bf(1.0 + 0.1 * np.random.standard_normal(D_MODEL)),
        "ln_b": bf(0.1 * np.random.standard_normal(D_MODEL)),
    }


def reference(attn_out, inp, w_proj1, w_proj2, ln_a, ln_b):
    o = f64(attn_out).reshape(H, T, D_V).transpose(1, 0, 2)
    o1 = o[:, :, :DV1].reshape(T, KP)
    o2 = o[:, :, DV1:].reshape(T, KP)
    y1 = mxq(o1, 1, "e4m3") @ mxq(f64(w_proj1), 0, "e4m3")
    y2 = mxq(o2, 1, "e4m3") @ mxq(f64(w_proj2), 0, "e4m3")
    z = np.concatenate([y1, y2], -1) + f64(inp)
    mu = np.mean(z, axis=-1, keepdims=True)
    sigma = np.std(z, axis=-1, keepdims=True, ddof=1)
    ln = (z - mu) / (sigma + EPS)
    return ln * f64(ln_a) + f64(ln_b)

@@ -1,0 +1,286 @@
+from contextlib import ExitStack
+
+import concourse.mybir as mybir
+from concourse.masks import make_identity
+
+F32 = mybir.dt.float32
+BF16 = mybir.dt.bfloat16
+U32 = mybir.dt.uint32
+U8 = mybir.dt.uint8
+FP8X4 = mybir.dt.float8_e4m3fn_x4
+ALU = mybir.AluOpType
+ACT = mybir.ActivationFunctionType
+
+P = 128
+HEADS = 8
+D_V = 128
+HALF = D_V // 2
+TOKENS = 1024
+K = HEADS * HALF
+N1 = 768
+N2 = 256
+D_MODEL = N1 + N2
+BANK = 512
+EPS = 1e-3
+TINY = 1e-30
+TILES = TOKENS // P
+
+TAIL_TILES = 2
+TAIL_V_COLS = 768
+
+FLOPS = 2 * TOKENS * K * D_MODEL
+
+
+def tile_multiheadattention_pa_kernel(tc, attn_out, inp, w_proj1, w_proj2, ln_a, ln_b, out):
+    nc = tc.nc
+    attn_tiles = attn_out.rearrange("h b l d -> h (b l) d").rearrange("h (k p) d -> k p h d", p=P)
+    inp_tiles = inp.rearrange("(k p) n -> k p n", p=P)
+    out_tiles = out.rearrange("(k p) n -> k p n", p=P)
+
+    with ExitStack() as ctx:
+        keep = ctx.enter_context(tc.tile_pool(name="keep", bufs=1))
+        loads = ctx.enter_context(tc.tile_pool(name="loads", bufs=TILES))
+        stage = ctx.enter_context(tc.tile_pool(name="stage", bufs=3))
+        work = ctx.enter_context(tc.tile_pool(name="work", bufs=3))
+        small = ctx.enter_context(tc.tile_pool(name="small", bufs=4))
+        gain_psum = ctx.enter_context(tc.psum_pool(name="gain_psum", bufs=1))
+        y_psum = ctx.enter_context(tc.psum_pool(name="y_psum", bufs=2))
+        t_psum = ctx.enter_context(tc.psum_pool(name="t_psum", bufs=2))
+        ctx.enter_context(tc.manual_schedule())
+
+        rows = keep.tile([P, 2 * D_MODEL], BF16)
+        nc.vector.memset(rows[:], 0.0)
+        ones = keep.tile([P, P], BF16)
+        nc.vector.memset(ones[:], 1.0)
+        one = keep.tile([P, 1], F32)
+        nc.vector.memset(one[:], 1.0)
+        warm = keep.tile([P, 1], F32)
+        nc.scalar.activation(out=warm[:], in_=one[:], func=ACT.Sqrt)
+        ident = keep.tile([P, P], F32)
+        make_identity(nc, ident[:])
+
+        x_raw = {}
+        inp_sb = {}
+
+        def load_attention(k):
+            x_k = loads.tile([P, HEADS, D_V], BF16, name="x_raw")
+            nc.sync.dma_start(out=x_k[:], in_=attn_tiles[k])
+            x_raw[k] = x_k
+
+        def load_residual(k):
+            inp_k = loads.tile([P, D_MODEL], BF16, name="inp_sb")
+            nc.sync.dma_start(out=inp_k[:], in_=inp_tiles[k])
+            inp_sb[k] = inp_k
+
+        load_attention(0)
+        w2_raw = keep.tile([P, 4, N2], BF16)
+        nc.sync.dma_start(out=w2_raw[:], in_=w_proj2.rearrange("(q t) n -> q t n", t=4))
+        w1_raw = keep.tile([P, 4, N1], BF16)
+        nc.sync.dma_start(out=w1_raw[:], in_=w_proj1.rearrange("(q t) n -> q t n", t=4))
+        nc.sync.dma_start(out=rows[0:1, 0:D_MODEL], in_=ln_a.unsqueeze(0))
+        nc.sync.dma_start(out=rows[0:1, D_MODEL : 2 * D_MODEL], in_=ln_b.unsqueeze(0))
+        load_residual(0)
+        load_attention(1)
+        load_attention(2)
+        for k in range(1, TILES):
+            load_residual(k)
+            if k + 2 < TILES:
+                load_attention(k + 2)
+
+        w_grouped = keep.tile([P, D_MODEL, 4], BF16, align_bytes=64)
+        w_codes = keep.tile([P, D_MODEL], U32, align_bytes=64)
+        w_scales = keep.tile([P, D_MODEL], U8, align_bytes=64)
+
+        def regroup_weight(copy, first, raw_cols):
+            width = raw_cols.shape[2]
+            copy(
+                out=w_grouped[:, first : first + width, :].rearrange("p (c i) t -> p c t i", i=4),
+                in_=raw_cols.rearrange("p t (c i) -> p c t i", i=4),
+            )
+
+        def quantise_weight(c):
+            cols = slice(c * BANK, (c + 1) * BANK)
+            nc.vector.quantize_mx(
+                out=w_codes[:, cols].bitcast(FP8X4),
+                scales=w_scales[:, cols],
+                in_=w_grouped[:, cols, :].rearrange("p n t -> p (n t)"),
+            )
+
+        o_codes = keep.tile([P, TILES, 2 * P], U32, align_bytes=64)
+        o_scales = keep.tile([P, TILES, 2 * P], U8, align_bytes=64)
+        x_split = {}
+        xt = {}
+        grouped = {}
+        y = {}
+        z = {}
+        sums = {}
+        neg_mean = {}
+        sum_sq = {}
+        sigma = {}
+        gained = {}
+        denom = {}
+        inv = {}
+
+        def sort_features(k):
+            split = stage.tile([P, 2, K], BF16, name="x_split")
+            nc.vector.tensor_copy(
+                out=split[:].rearrange("p s (h j) -> p s h j", j=HALF),
+                in_=x_raw[k][:].rearrange("p h (s j) -> p s h j", s=2),
+            )
+            x_split[k] = split
+
+        def flip(k):
+            words = x_split[k][:].bitcast(F32)
+            planes = t_psum.tile([P, 2, 2, P], F32, name="xt")
+            for s in range(2):
+                for u in range(2):
+                    nc.tensor.transpose(planes[:, s, u, :], words[:, s, u : 2 * P : 2], ident[:])
+            xt[k] = planes
+
+        def evacuate(k):
+            packed = stage.tile([P, 2, P, 4], BF16, align_bytes=64, name="grouped")
+            nc.scalar.copy(out=packed[:].bitcast(F32), in_=xt[k][:].rearrange("p s u m -> p s m u"))
+            grouped[k] = packed
+
+        def quantise(k):
+            nc.vector.quantize_mx(
+                out=o_codes[:, k, :].bitcast(FP8X4),
+                scales=o_scales[:, k, :],
+                in_=grouped[k][:].rearrange("p s m t -> p (s m t)"),
+            )
+
+        def project(k):
+            def mx(acc, s, cols):
+                nc.tensor.matmul_mx(
+                    out=acc,
+                    lhsT=o_codes[:, k, s * P : (s + 1) * P].bitcast(FP8X4),
+                    lhsT_scale=o_scales[:, k, s * P : (s + 1) * P],
+                    rhs=w_codes[:, cols].bitcast(FP8X4),
+                    rhs_scale=w_scales[:, cols],
+                    start=True,
+                    stop=True,
+                )
+
+            y0 = y_psum.tile([P, BANK], F32)
+            y1 = y_psum.tile([P, BANK], F32)
+            mx(y0[:], 0, slice(0, BANK))
+            mx(y1[:, 0 : N1 - BANK], 0, slice(BANK, N1))
+            mx(y1[:, N1 - BANK : BANK], 1, slice(N1, D_MODEL))
+            y[k] = [y0, y1]
+
+        def add_residual(k):
+            z_k = work.tile([P, D_MODEL], F32, name="z")
+            sums_k = small.tile([P, 2], F32, name="sums")
+            for c in range(2):
+                cols = slice(c * BANK, (c + 1) * BANK)
+                nc.vector.scalar_tensor_tensor(
+                    out=z_k[:, cols], in0=y[k][c][:], scalar=1.0, in1=inp_sb[k][:, cols],
+                    op0=ALU.mult, op1=ALU.add, accum_out=sums_k[:, c : c + 1],
+                )
+            z[k] = z_k
+            sums[k] = sums_k
+
+        def mean(k):
+            neg = small.tile([P, 1], F32, name="neg_mean")
+            nc.vector.tensor_scalar(
+                out=neg[:], in0=sums[k][:, 0:1], scalar1=sums[k][:, 1:2], scalar2=-1.0 / D_MODEL, op0=ALU.add, op1=ALU.mult
+            )
+            neg_mean[k] = neg
+
+        def squares(k):
+            unused = work.tile([P, D_MODEL], BF16, name="squares")
+            total = small.tile([P, 1], F32, name="sum_sq")
+            nc.scalar.activation(out=unused[:], in_=z[k][:], func=ACT.Square, bias=neg_mean[k][:], scale=1.0, accum_out=total[:])
+            sum_sq[k] = total
+
+        def root(k):
+            sigma_k = small.tile([P, 1], F32, name="sigma")
+            nc.scalar.activation(out=sigma_k[:], in_=sum_sq[k][:], func=ACT.Sqrt, bias=TINY, scale=1.0 / (D_MODEL - 1))
+            sigma[k] = sigma_k
+
+        def apply_gain(k, c):
+            cols = slice(c * BANK, (c + 1) * BANK)
+            nc.vector.scalar_tensor_tensor(
+                out=gained[k][:, cols], in0=z[k][:, cols], scalar=neg_mean[k][:], in1=gain[c][:], op0=ALU.add, op1=ALU.mult
+            )
+
+        def gain_low(k):
+            gained_k = work.tile([P, D_MODEL], F32, name="gained")
+            gained[k] = gained_k
+            apply_gain(k, 0)
+
+        def gain_high(k):
+            apply_gain(k, 1)
+
+        def add_eps(k):
+            denom_k = small.tile([P, 1], F32, name="denom")
+            nc.vector.tensor_scalar_add(out=denom_k[:], in0=sigma[k][:], scalar1=EPS)
+            denom[k] = denom_k
+
+        def invert(k):
+            inv_k = small.tile([P, 1], F32, name="inv")
+            nc.vector.reciprocal(out=inv_k[:], in_=denom[k][:])
+            inv[k] = inv_k
+
+        def finish(k):
+            v_cols = TAIL_V_COLS if k >= TILES - TAIL_TILES else 0
+            result = work.tile([P, D_MODEL], F32)
+            if v_cols > 0:
+                nc.vector.scalar_tensor_tensor(
+                    out=result[:, :v_cols], in0=gained[k][:, :v_cols], scalar=inv[k][:], in1=bias[:, :v_cols],
+                    op0=ALU.mult, op1=ALU.add,
+                )
+            scaled = work.tile([P, D_MODEL], F32)
+            nc.scalar.activation(out=scaled[:, v_cols:], in_=gained[k][:, v_cols:], func=ACT.Copy, scale=inv[k][:])
+            nc.gpsimd.tensor_tensor(out=result[:, v_cols:], in0=scaled[:, v_cols:], in1=bias[:, v_cols:], op=ALU.add)
+            nc.sync.dma_start(out=out_tiles[k], in_=result[:])
+
+        sort_features(0)
+        flip(0)
+        evacuate(0)
+        regroup_weight(nc.vector.tensor_copy, N1, w2_raw[:])
+        quantise(0)
+        regroup_weight(nc.vector.tensor_copy, 0, w1_raw[:, :, 0:BANK])
+        regroup_weight(nc.scalar.copy, BANK, w1_raw[:, :, BANK:N1])
+        gain = []
+        for c in range(2):
+            gain_c = gain_psum.tile([P, BANK], F32, name="gain%d" % c)
+            nc.tensor.matmul(out=gain_c[:], lhsT=ones[:], rhs=rows[:, c * BANK : (c + 1) * BANK], start=True, stop=True)
+            gain.append(gain_c)
+        bias = keep.tile([P, D_MODEL], F32)
+        for c in range(2):
+            bias_c = y_psum.tile([P, BANK], F32, tag="y%d" % c)
+            nc.tensor.matmul(
+                out=bias_c[:], lhsT=ones[:], rhs=rows[:, D_MODEL + c * BANK : D_MODEL + (c + 1) * BANK], start=True, stop=True
+            )
+            nc.scalar.copy(out=bias[:, c * BANK : (c + 1) * BANK], in_=bias_c[:])
+        quantise_weight(0)
+        quantise_weight(1)
+        project(0)
+        for k in range(1, 3):
+            sort_features(k)
+            flip(k)
+            evacuate(k)
+
+        def at(k, stage_of):
+            if 0 <= k < TILES:
+                stage_of(k)
+
+        projected = 1
+        for k in range(TILES + 1):
+            at(k, add_residual)
+            at(k + 3, sort_features)
+            at(k, mean)
+            at(k, squares)
+            at(k + 3, flip)
+            while projected <= min(k + 2, TILES - 1):
+                quantise(projected)
+                project(projected)
+                projected += 1
+            at(k, gain_low)
+            at(k - 1, add_eps)
+            at(k, gain_high)
+            at(k - 1, invert)
+            at(k + 3, evacuate)
+            at(k, root)
+            at(k - 1, finish)

@@ -43,7 +43,7 @@ def tile_multiheadattention_pa_kernel(tc, attn_out, inp, w_proj1, w_proj2, ln_a,
         stage = ctx.enter_context(tc.tile_pool(name="stage", bufs=3))
         work = ctx.enter_context(tc.tile_pool(name="work", bufs=3))
         small = ctx.enter_context(tc.tile_pool(name="small", bufs=4))
-        gain_psum = ctx.enter_context(tc.psum_pool(name="gain_psum", bufs=1))
+        row_psum = ctx.enter_context(tc.psum_pool(name="row_psum", bufs=1))
         y_psum = ctx.enter_context(tc.psum_pool(name="y_psum", bufs=2))
         t_psum = ctx.enter_context(tc.psum_pool(name="t_psum", bufs=2))
         ctx.enter_context(tc.manual_schedule())
@@ -198,19 +198,12 @@ def tile_multiheadattention_pa_kernel(tc, attn_out, inp, w_proj1, w_proj2, ln_a,
             nc.scalar.activation(out=sigma_k[:], in_=sum_sq[k][:], func=ACT.Sqrt, bias=TINY, scale=1.0 / (D_MODEL - 1))
             sigma[k] = sigma_k
 
-        def apply_gain(k, c):
-            cols = slice(c * BANK, (c + 1) * BANK)
-            nc.vector.scalar_tensor_tensor(
-                out=gained[k][:, cols], in0=z[k][:, cols], scalar=neg_mean[k][:], in1=gain[c][:], op0=ALU.add, op1=ALU.mult
-            )
-
-        def gain_low(k):
+        def apply_gain(k):
             gained_k = work.tile([P, D_MODEL], F32, name="gained")
+            nc.vector.scalar_tensor_tensor(
+                out=gained_k[:], in0=z[k][:], scalar=neg_mean[k][:], in1=gain[:], op0=ALU.add, op1=ALU.mult
+            )
             gained[k] = gained_k
-            apply_gain(k, 0)
-
-        def gain_high(k):
-            apply_gain(k, 1)
 
         def add_eps(k):
             denom_k = small.tile([P, 1], F32, name="denom")
@@ -242,18 +235,19 @@ def tile_multiheadattention_pa_kernel(tc, attn_out, inp, w_proj1, w_proj2, ln_a,
         quantise(0)
         regroup_weight(nc.vector.tensor_copy, 0, w1_raw[:, :, 0:BANK])
         regroup_weight(nc.scalar.copy, BANK, w1_raw[:, :, BANK:N1])
-        gain = []
-        for c in range(2):
-            gain_c = gain_psum.tile([P, BANK], F32, name="gain%d" % c)
-            nc.tensor.matmul(out=gain_c[:], lhsT=ones[:], rhs=rows[:, c * BANK : (c + 1) * BANK], start=True, stop=True)
-            gain.append(gain_c)
-        bias = keep.tile([P, D_MODEL], F32)
-        for c in range(2):
-            bias_c = y_psum.tile([P, BANK], F32, tag="y%d" % c)
-            nc.tensor.matmul(
-                out=bias_c[:], lhsT=ones[:], rhs=rows[:, D_MODEL + c * BANK : D_MODEL + (c + 1) * BANK], start=True, stop=True
-            )
-            nc.scalar.copy(out=bias[:, c * BANK : (c + 1) * BANK], in_=bias_c[:])
+        def repeat_row(first, spread):
+            for c in range(2):
+                cols = slice(c * BANK, (c + 1) * BANK)
+                nc.tensor.matmul(
+                    out=spread[:, cols], lhsT=ones[:], rhs=rows[:, first + c * BANK : first + (c + 1) * BANK], start=True, stop=True
+                )
+
+        gain = row_psum.tile([P, D_MODEL], BF16)
+        repeat_row(0, gain)
+        bias_psum = row_psum.tile([P, D_MODEL], BF16)
+        repeat_row(D_MODEL, bias_psum)
+        bias = keep.tile([P, D_MODEL], BF16)
+        nc.scalar.copy(out=bias[:], in_=bias_psum[:])
         quantise_weight(0)
         quantise_weight(1)
         project(0)
@@ -277,9 +271,8 @@ def tile_multiheadattention_pa_kernel(tc, attn_out, inp, w_proj1, w_proj2, ln_a,
                 quantise(projected)
                 project(projected)
                 projected += 1
-            at(k, gain_low)
             at(k - 1, add_eps)
-            at(k, gain_high)
+            at(k, apply_gain)
             at(k - 1, invert)
             at(k + 3, evacuate)
             at(k, root)

@@ -25,6 +25,8 @@ EPS = 1e-3
 TINY = 1e-30
 TILES = TOKENS // P
 
+GROUPS = (1, 1, 2, 4)
+
 TAIL_TILES = 2
 TAIL_V_COLS = 768
 
@@ -33,13 +35,10 @@ FLOPS = 2 * TOKENS * K * D_MODEL
 
 def tile_multiheadattention_pa_kernel(tc, attn_out, inp, w_proj1, w_proj2, ln_a, ln_b, out):
     nc = tc.nc
-    attn_tiles = attn_out.rearrange("h b l d -> h (b l) d").rearrange("h (k p) d -> k p h d", p=P)
-    inp_tiles = inp.rearrange("(k p) n -> k p n", p=P)
-    out_tiles = out.rearrange("(k p) n -> k p n", p=P)
+    attn = attn_out.rearrange("h b l d -> h (b l) d")
 
     with ExitStack() as ctx:
         keep = ctx.enter_context(tc.tile_pool(name="keep", bufs=1))
-        loads = ctx.enter_context(tc.tile_pool(name="loads", bufs=TILES))
         stage = ctx.enter_context(tc.tile_pool(name="stage", bufs=3))
         work = ctx.enter_context(tc.tile_pool(name="work", bufs=3))
         small = ctx.enter_context(tc.tile_pool(name="small", bufs=4))
@@ -61,31 +60,51 @@ def tile_multiheadattention_pa_kernel(tc, attn_out, inp, w_proj1, w_proj2, ln_a,
 
         x_raw = {}
         inp_sb = {}
+        out_rows = {}
+        group_of = []
+        first = 0
+        for g, width in enumerate(GROUPS):
+            tokens = slice(first * P, (first + width) * P)
+            group_of.append((first, width, tokens))
+            for j in range(width):
+                out_rows[first + j] = out[tokens, :].rearrange("(p j) n -> p j n", j=width)[:, j, :]
+            first += width
 
-        def load_attention(k):
-            x_k = loads.tile([P, HEADS, D_V], BF16, name="x_raw")
-            nc.sync.dma_start(out=x_k[:], in_=attn_tiles[k])
-            x_raw[k] = x_k
+        def load_attention(g):
+            start, width, tokens = group_of[g]
+            x_g = keep.tile([P, HEADS, width, D_V], BF16, name="x_raw%d" % g)
+            nc.sync.dma_start(
+                out=x_g[:].rearrange("p h j d -> p h (j d)"),
+                in_=attn[:, tokens, :].rearrange("h (p j) d -> p h (j d)", j=width),
+            )
+            for j in range(width):
+                x_raw[start + j] = x_g[:, :, j, :]
 
-        def load_residual(k):
-            inp_k = loads.tile([P, D_MODEL], BF16, name="inp_sb")
-            nc.sync.dma_start(out=inp_k[:], in_=inp_tiles[k])
-            inp_sb[k] = inp_k
+        def load_residual(g, low, high):
+            start, width, tokens = group_of[g]
+            inp_g = keep.tile([P, high - low, D_MODEL], BF16, name="inp%d_%d" % (g, low))
+            nc.sync.dma_start(out=inp_g[:], in_=inp[tokens, :].rearrange("(p j) n -> p j n", j=width)[:, low:high, :])
+            for j in range(low, high):
+                inp_sb[start + j] = inp_g[:, j - low, :]
 
         load_attention(0)
-        w2_raw = keep.tile([P, 4, N2], BF16)
-        nc.sync.dma_start(out=w2_raw[:], in_=w_proj2.rearrange("(q t) n -> q t n", t=4))
-        w1_raw = keep.tile([P, 4, N1], BF16)
-        nc.sync.dma_start(out=w1_raw[:], in_=w_proj1.rearrange("(q t) n -> q t n", t=4))
+        w1_rows = w_proj1.rearrange("(q t) n -> q t n", t=4)
+        w1_low = keep.tile([P, 4, BANK], BF16)
+        nc.sync.dma_start(out=w1_low[:], in_=w1_rows[:, :, 0:BANK])
         nc.sync.dma_start(out=rows[0:1, 0:D_MODEL], in_=ln_a.unsqueeze(0))
         nc.sync.dma_start(out=rows[0:1, D_MODEL : 2 * D_MODEL], in_=ln_b.unsqueeze(0))
-        load_residual(0)
+        w1_high = keep.tile([P, 4, N1 - BANK], BF16)
+        nc.sync.dma_start(out=w1_high[:], in_=w1_rows[:, :, BANK:N1])
+        w2_raw = keep.tile([P, 4, N2], BF16)
+        nc.sync.dma_start(out=w2_raw[:], in_=w_proj2.rearrange("(q t) n -> q t n", t=4))
         load_attention(1)
+        load_residual(0, 0, 1)
         load_attention(2)
-        for k in range(1, TILES):
-            load_residual(k)
-            if k + 2 < TILES:
-                load_attention(k + 2)
+        load_residual(1, 0, 1)
+        load_attention(3)
+        load_residual(2, 0, 2)
+        load_residual(3, 0, 2)
+        load_residual(3, 2, 4)
 
         w_grouped = keep.tile([P, D_MODEL, 4], BF16, align_bytes=64)
         w_codes = keep.tile([P, D_MODEL], U32, align_bytes=64)
@@ -125,7 +144,7 @@ def tile_multiheadattention_pa_kernel(tc, attn_out, inp, w_proj1, w_proj2, ln_a,
             split = stage.tile([P, 2, K], BF16, name="x_split")
             nc.vector.tensor_copy(
                 out=split[:].rearrange("p s (h j) -> p s h j", j=HALF),
-                in_=x_raw[k][:].rearrange("p h (s j) -> p s h j", s=2),
+                in_=x_raw[k].rearrange("p h (s j) -> p s h j", s=2),
             )
             x_split[k] = split
 
@@ -149,7 +168,7 @@ def tile_multiheadattention_pa_kernel(tc, attn_out, inp, w_proj1, w_proj2, ln_a,
                 in_=grouped[k][:].rearrange("p s m t -> p (s m t)"),
             )
 
-        def project(k):
+        def project(k, c):
             def mx(acc, s, cols):
                 nc.tensor.matmul_mx(
                     out=acc,
@@ -161,12 +180,13 @@ def tile_multiheadattention_pa_kernel(tc, attn_out, inp, w_proj1, w_proj2, ln_a,
                     stop=True,
                 )
 
-            y0 = y_psum.tile([P, BANK], F32)
-            y1 = y_psum.tile([P, BANK], F32)
-            mx(y0[:], 0, slice(0, BANK))
-            mx(y1[:, 0 : N1 - BANK], 0, slice(BANK, N1))
-            mx(y1[:, N1 - BANK : BANK], 1, slice(N1, D_MODEL))
-            y[k] = [y0, y1]
+            bank = y_psum.tile([P, BANK], F32, name="y%d" % c)
+            if c == 0:
+                mx(bank[:], 0, slice(0, BANK))
+            else:
+                mx(bank[:, 0 : N1 - BANK], 0, slice(BANK, N1))
+                mx(bank[:, N1 - BANK : BANK], 1, slice(N1, D_MODEL))
+            y[k, c] = bank
 
         def add_residual(k):
             z_k = work.tile([P, D_MODEL], F32, name="z")
@@ -174,7 +194,7 @@ def tile_multiheadattention_pa_kernel(tc, attn_out, inp, w_proj1, w_proj2, ln_a,
             for c in range(2):
                 cols = slice(c * BANK, (c + 1) * BANK)
                 nc.vector.scalar_tensor_tensor(
-                    out=z_k[:, cols], in0=y[k][c][:], scalar=1.0, in1=inp_sb[k][:, cols],
+                    out=z_k[:, cols], in0=y[k, c][:], scalar=1.0, in1=inp_sb[k][:, cols],
                     op0=ALU.mult, op1=ALU.add, accum_out=sums_k[:, c : c + 1],
                 )
             z[k] = z_k
@@ -226,15 +246,12 @@ def tile_multiheadattention_pa_kernel(tc, attn_out, inp, w_proj1, w_proj2, ln_a,
             scaled = work.tile([P, D_MODEL], F32)
             nc.scalar.activation(out=scaled[:, v_cols:], in_=gained[k][:, v_cols:], func=ACT.Copy, scale=inv[k][:])
             nc.gpsimd.tensor_tensor(out=result[:, v_cols:], in0=scaled[:, v_cols:], in1=bias[:, v_cols:], op=ALU.add)
-            nc.sync.dma_start(out=out_tiles[k], in_=result[:])
+            nc.sync.dma_start(out=out_rows[k], in_=result[:])
 
         sort_features(0)
         flip(0)
         evacuate(0)
-        regroup_weight(nc.vector.tensor_copy, N1, w2_raw[:])
-        quantise(0)
-        regroup_weight(nc.vector.tensor_copy, 0, w1_raw[:, :, 0:BANK])
-        regroup_weight(nc.scalar.copy, BANK, w1_raw[:, :, BANK:N1])
+
         def repeat_row(first, spread):
             for c in range(2):
                 cols = slice(c * BANK, (c + 1) * BANK)
@@ -246,15 +263,22 @@ def tile_multiheadattention_pa_kernel(tc, attn_out, inp, w_proj1, w_proj2, ln_a,
         repeat_row(0, gain)
         bias_psum = row_psum.tile([P, D_MODEL], BF16)
         repeat_row(D_MODEL, bias_psum)
+        regroup_weight(nc.vector.tensor_copy, 0, w1_low[:])
+        regroup_weight(nc.scalar.copy, BANK, w1_high[:])
+        quantise(0)
+        quantise_weight(0)
+        project(0, 0)
+        sort_features(1)
+        flip(1)
+        regroup_weight(nc.vector.tensor_copy, N1, w2_raw[:])
+        quantise_weight(1)
+        project(0, 1)
         bias = keep.tile([P, D_MODEL], BF16)
         nc.scalar.copy(out=bias[:], in_=bias_psum[:])
-        quantise_weight(0)
-        quantise_weight(1)
-        project(0)
-        for k in range(1, 3):
-            sort_features(k)
-            flip(k)
-            evacuate(k)
+        evacuate(1)
+        sort_features(2)
+        flip(2)
+        evacuate(2)
 
         def at(k, stage_of):
             if 0 <= k < TILES:
@@ -269,7 +293,8 @@ def tile_multiheadattention_pa_kernel(tc, attn_out, inp, w_proj1, w_proj2, ln_a,
             at(k + 3, flip)
             while projected <= min(k + 2, TILES - 1):
                 quantise(projected)
-                project(projected)
+                project(projected, 0)
+                project(projected, 1)
                 projected += 1
             at(k - 1, add_eps)
             at(k, apply_gain)

@@ -25,8 +25,6 @@ EPS = 1e-3
 TINY = 1e-30
 TILES = TOKENS // P
 
-GROUPS = (1, 1, 2, 4)
-
 TAIL_TILES = 2
 TAIL_V_COLS = 768
 
@@ -39,12 +37,13 @@ def tile_multiheadattention_pa_kernel(tc, attn_out, inp, w_proj1, w_proj2, ln_a,
 
     with ExitStack() as ctx:
         keep = ctx.enter_context(tc.tile_pool(name="keep", bufs=1))
+        splits = ctx.enter_context(tc.tile_pool(name="splits", bufs=4))
         stage = ctx.enter_context(tc.tile_pool(name="stage", bufs=3))
-        work = ctx.enter_context(tc.tile_pool(name="work", bufs=3))
-        small = ctx.enter_context(tc.tile_pool(name="small", bufs=4))
-        row_psum = ctx.enter_context(tc.psum_pool(name="row_psum", bufs=1))
+        work = ctx.enter_context(tc.tile_pool(name="work", bufs=TILES))
+        small = ctx.enter_context(tc.tile_pool(name="small", bufs=TILES))
+        gain_psum = ctx.enter_context(tc.psum_pool(name="gain_psum", bufs=1))
         y_psum = ctx.enter_context(tc.psum_pool(name="y_psum", bufs=2))
-        t_psum = ctx.enter_context(tc.psum_pool(name="t_psum", bufs=2))
+        t_psum = ctx.enter_context(tc.psum_pool(name="t_psum", bufs=3))
         ctx.enter_context(tc.manual_schedule())
 
         rows = keep.tile([P, 2 * D_MODEL], BF16)
@@ -59,35 +58,44 @@ def tile_multiheadattention_pa_kernel(tc, attn_out, inp, w_proj1, w_proj2, ln_a,
         make_identity(nc, ident[:])
 
         x_raw = {}
+        x_split = {}
         inp_sb = {}
         out_rows = {}
-        group_of = []
-        first = 0
-        for g, width in enumerate(GROUPS):
+
+        def group(first, width):
             tokens = slice(first * P, (first + width) * P)
-            group_of.append((first, width, tokens))
             for j in range(width):
                 out_rows[first + j] = out[tokens, :].rearrange("(p j) n -> p j n", j=width)[:, j, :]
-            first += width
+            return tokens
 
-        def load_attention(g):
-            start, width, tokens = group_of[g]
-            x_g = keep.tile([P, HEADS, width, D_V], BF16, name="x_raw%d" % g)
+        def load_attention(first, width):
+            tokens = group(first, width)
+            x_g = keep.tile([P, HEADS, width, D_V], BF16, name="x_raw%d" % first)
             nc.sync.dma_start(
                 out=x_g[:].rearrange("p h j d -> p h (j d)"),
                 in_=attn[:, tokens, :].rearrange("h (p j) d -> p h (j d)", j=width),
             )
             for j in range(width):
-                x_raw[start + j] = x_g[:, :, j, :]
+                x_raw[first + j] = x_g[:, :, j, :]
 
-        def load_residual(g, low, high):
-            start, width, tokens = group_of[g]
-            inp_g = keep.tile([P, high - low, D_MODEL], BF16, name="inp%d_%d" % (g, low))
-            nc.sync.dma_start(out=inp_g[:], in_=inp[tokens, :].rearrange("(p j) n -> p j n", j=width)[:, low:high, :])
-            for j in range(low, high):
-                inp_sb[start + j] = inp_g[:, j - low, :]
+        def load_sorted_attention(k):
+            tokens = group(k, 1)
+            split = keep.tile([P, 2, K], BF16, name="x_sorted%d" % k)
+            for s in range(2):
+                nc.sync.dma_start(
+                    out=split[:, s, :].rearrange("p (h j) -> p h j", j=HALF),
+                    in_=attn[:, tokens, s * HALF : (s + 1) * HALF].rearrange("h p j -> p h j"),
+                )
+            x_split[k] = split
 
-        load_attention(0)
+        def load_residual(first, width):
+            tokens = slice(first * P, (first + width) * P)
+            inp_g = keep.tile([P, width, D_MODEL], BF16, name="inp%d" % first)
+            nc.sync.dma_start(out=inp_g[:], in_=inp[tokens, :].rearrange("(p j) n -> p j n", j=width))
+            for j in range(width):
+                inp_sb[first + j] = inp_g[:, j, :]
+
+        load_attention(0, 1)
         w1_rows = w_proj1.rearrange("(q t) n -> q t n", t=4)
         w1_low = keep.tile([P, 4, BANK], BF16)
         nc.sync.dma_start(out=w1_low[:], in_=w1_rows[:, :, 0:BANK])
@@ -97,14 +105,19 @@ def tile_multiheadattention_pa_kernel(tc, attn_out, inp, w_proj1, w_proj2, ln_a,
         nc.sync.dma_start(out=w1_high[:], in_=w1_rows[:, :, BANK:N1])
         w2_raw = keep.tile([P, 4, N2], BF16)
         nc.sync.dma_start(out=w2_raw[:], in_=w_proj2.rearrange("(q t) n -> q t n", t=4))
-        load_attention(1)
-        load_residual(0, 0, 1)
-        load_attention(2)
-        load_residual(1, 0, 1)
-        load_attention(3)
-        load_residual(2, 0, 2)
-        load_residual(3, 0, 2)
-        load_residual(3, 2, 4)
+        load_attention(1, 1)
+        load_residual(0, 1)
+        load_attention(2, 2)
+        load_residual(1, 1)
+        load_attention(4, 1)
+        load_residual(2, 2)
+        load_sorted_attention(5)
+        load_residual(4, 1)
+        load_sorted_attention(6)
+        load_residual(5, 1)
+        load_sorted_attention(7)
+        load_residual(6, 1)
+        load_residual(7, 1)
 
         w_grouped = keep.tile([P, D_MODEL, 4], BF16, align_bytes=64)
         w_codes = keep.tile([P, D_MODEL], U32, align_bytes=64)
@@ -127,7 +140,6 @@ def tile_multiheadattention_pa_kernel(tc, attn_out, inp, w_proj1, w_proj2, ln_a,
 
         o_codes = keep.tile([P, TILES, 2 * P], U32, align_bytes=64)
         o_scales = keep.tile([P, TILES, 2 * P], U8, align_bytes=64)
-        x_split = {}
         xt = {}
         grouped = {}
         y = {}
@@ -139,9 +151,10 @@ def tile_multiheadattention_pa_kernel(tc, attn_out, inp, w_proj1, w_proj2, ln_a,
         gained = {}
         denom = {}
         inv = {}
+        result = {}
 
         def sort_features(k):
-            split = stage.tile([P, 2, K], BF16, name="x_split")
+            split = splits.tile([P, 2, K], BF16, name="x_split")
             nc.vector.tensor_copy(
                 out=split[:].rearrange("p s (h j) -> p s h j", j=HALF),
                 in_=x_raw[k].rearrange("p h (s j) -> p s h j", s=2),
@@ -235,18 +248,23 @@ def tile_multiheadattention_pa_kernel(tc, attn_out, inp, w_proj1, w_proj2, ln_a,
             nc.vector.reciprocal(out=inv_k[:], in_=denom[k][:])
             inv[k] = inv_k
 
+        def store(k, low, high):
+            nc.sync.dma_start(out=out_rows[k][:, low:high], in_=result[k][:, low:high])
+
         def finish(k):
             v_cols = TAIL_V_COLS if k >= TILES - TAIL_TILES else 0
-            result = work.tile([P, D_MODEL], F32)
+            result_k = work.tile([P, D_MODEL], F32, name="result")
+            result[k] = result_k
             if v_cols > 0:
                 nc.vector.scalar_tensor_tensor(
-                    out=result[:, :v_cols], in0=gained[k][:, :v_cols], scalar=inv[k][:], in1=bias[:, :v_cols],
+                    out=result_k[:, :v_cols], in0=gained[k][:, :v_cols], scalar=inv[k][:], in1=bias[:, :v_cols],
                     op0=ALU.mult, op1=ALU.add,
                 )
+                store(k, 0, v_cols)
             scaled = work.tile([P, D_MODEL], F32)
             nc.scalar.activation(out=scaled[:, v_cols:], in_=gained[k][:, v_cols:], func=ACT.Copy, scale=inv[k][:])
-            nc.gpsimd.tensor_tensor(out=result[:, v_cols:], in0=scaled[:, v_cols:], in1=bias[:, v_cols:], op=ALU.add)
-            nc.sync.dma_start(out=out_rows[k], in_=result[:])
+            nc.gpsimd.tensor_tensor(out=result_k[:, v_cols:], in0=scaled[:, v_cols:], in1=bias[:, v_cols:], op=ALU.add)
+            store(k, v_cols, D_MODEL)
 
         sort_features(0)
         flip(0)
@@ -259,46 +277,48 @@ def tile_multiheadattention_pa_kernel(tc, attn_out, inp, w_proj1, w_proj2, ln_a,
                     out=spread[:, cols], lhsT=ones[:], rhs=rows[:, first + c * BANK : first + (c + 1) * BANK], start=True, stop=True
                 )
 
-        gain = row_psum.tile([P, D_MODEL], BF16)
+        gain = gain_psum.tile([P, D_MODEL], BF16)
         repeat_row(0, gain)
-        bias_psum = row_psum.tile([P, D_MODEL], BF16)
+        bias_psum = t_psum.tile([P, D_MODEL], BF16, name="xt")
         repeat_row(D_MODEL, bias_psum)
         regroup_weight(nc.vector.tensor_copy, 0, w1_low[:])
         regroup_weight(nc.scalar.copy, BANK, w1_high[:])
         quantise(0)
         quantise_weight(0)
         project(0, 0)
+        regroup_weight(nc.vector.tensor_copy, N1, w2_raw[:])
         sort_features(1)
         flip(1)
-        regroup_weight(nc.vector.tensor_copy, N1, w2_raw[:])
         quantise_weight(1)
         project(0, 1)
         bias = keep.tile([P, D_MODEL], BF16)
         nc.scalar.copy(out=bias[:], in_=bias_psum[:])
         evacuate(1)
-        sort_features(2)
-        flip(2)
-        evacuate(2)
 
-        def at(k, stage_of):
+        def at(k, stage_of, *args):
             if 0 <= k < TILES:
-                stage_of(k)
+                stage_of(k, *args)
 
-        projected = 1
         for k in range(TILES + 1):
             at(k, add_residual)
-            at(k + 3, sort_features)
+            if k == TILES:
+                apply_gain(k - 1)
+            at(k - 1, add_eps)
+            at(k + 1, quantise)
+            at(k + 1, project, 0)
+            at(k + 1, project, 1)
             at(k, mean)
             at(k, squares)
-            at(k + 3, flip)
-            while projected <= min(k + 2, TILES - 1):
-                quantise(projected)
-                project(projected, 0)
-                project(projected, 1)
-                projected += 1
-            at(k - 1, add_eps)
-            at(k, apply_gain)
+            if k == 0:
+                for t in (2, 3):
+                    sort_features(t)
+                    flip(t)
+            at(k + 2, evacuate)
+            if 4 <= k + 4 < 5:
+                sort_features(k + 4)
+            at(k + 4, flip)
             at(k - 1, invert)
-            at(k + 3, evacuate)
+            if k < TILES:
+                at(k - 1, apply_gain)
             at(k, root)
             at(k - 1, finish)

@@ -207,7 +207,7 @@ def tile_multiheadattention_pa_kernel(tc, attn_out, inp, w_proj1, w_proj2, ln_a,
             for c in range(2):
                 cols = slice(c * BANK, (c + 1) * BANK)
                 nc.vector.scalar_tensor_tensor(
-                    out=z_k[:, cols], in0=y[k, c][:], scalar=1.0, in1=inp_sb[k][:, cols],
+                    out=z_k[:, cols], in0=inp_sb[k][:, cols], scalar=1.0, in1=y[k, c][:],
                     op0=ALU.mult, op1=ALU.add, accum_out=sums_k[:, c : c + 1],
                 )
             z[k] = z_k

@@ -25,8 +25,8 @@ EPS = 1e-3
 TINY = 1e-30
 TILES = TOKENS // P
 
-TAIL_TILES = 2
-TAIL_V_COLS = 768
+TAIL_TILES = 3
+RAMP = 256
 
 FLOPS = 2 * TOKENS * K * D_MODEL
 
@@ -41,9 +41,9 @@ def tile_multiheadattention_pa_kernel(tc, attn_out, inp, w_proj1, w_proj2, ln_a,
         stage = ctx.enter_context(tc.tile_pool(name="stage", bufs=3))
         work = ctx.enter_context(tc.tile_pool(name="work", bufs=TILES))
         small = ctx.enter_context(tc.tile_pool(name="small", bufs=TILES))
-        gain_psum = ctx.enter_context(tc.psum_pool(name="gain_psum", bufs=1))
+        row_psum = ctx.enter_context(tc.psum_pool(name="row_psum", bufs=1))
         y_psum = ctx.enter_context(tc.psum_pool(name="y_psum", bufs=2))
-        t_psum = ctx.enter_context(tc.psum_pool(name="t_psum", bufs=3))
+        t_psum = ctx.enter_context(tc.psum_pool(name="t_psum", bufs=2))
         ctx.enter_context(tc.manual_schedule())
 
         rows = keep.tile([P, 2 * D_MODEL], BF16)
@@ -252,12 +252,12 @@ def tile_multiheadattention_pa_kernel(tc, attn_out, inp, w_proj1, w_proj2, ln_a,
             nc.sync.dma_start(out=out_rows[k][:, low:high], in_=result[k][:, low:high])
 
         def finish(k):
-            v_cols = TAIL_V_COLS if k >= TILES - TAIL_TILES else 0
+            v_cols = max(0, RAMP * (k + 1 - (TILES - TAIL_TILES)))
             result_k = work.tile([P, D_MODEL], F32, name="result")
             result[k] = result_k
             if v_cols > 0:
                 nc.vector.scalar_tensor_tensor(
-                    out=result_k[:, :v_cols], in0=gained[k][:, :v_cols], scalar=inv[k][:], in1=bias[:, :v_cols],
+                    out=result_k[:, :v_cols], in0=gained[k][:, :v_cols], scalar=inv[k][:], in1=bias_psum[:, :v_cols],
                     op0=ALU.mult, op1=ALU.add,
                 )
                 store(k, 0, v_cols)
@@ -277,9 +277,9 @@ def tile_multiheadattention_pa_kernel(tc, attn_out, inp, w_proj1, w_proj2, ln_a,
                     out=spread[:, cols], lhsT=ones[:], rhs=rows[:, first + c * BANK : first + (c + 1) * BANK], start=True, stop=True
                 )
 
-        gain = gain_psum.tile([P, D_MODEL], BF16)
+        gain = row_psum.tile([P, D_MODEL], BF16)
         repeat_row(0, gain)
-        bias_psum = t_psum.tile([P, D_MODEL], BF16, name="xt")
+        bias_psum = row_psum.tile([P, D_MODEL], BF16)
         repeat_row(D_MODEL, bias_psum)
         regroup_weight(nc.vector.tensor_copy, 0, w1_low[:])
         regroup_weight(nc.scalar.copy, BANK, w1_high[:])

from contextlib import ExitStack

import concourse.mybir as mybir
from concourse.masks import make_identity

F32 = mybir.dt.float32
BF16 = mybir.dt.bfloat16
U32 = mybir.dt.uint32
U8 = mybir.dt.uint8
FP8X4 = mybir.dt.float8_e4m3fn_x4
ALU = mybir.AluOpType
ACT = mybir.ActivationFunctionType

P = 128
HEADS = 8
D_V = 128
HALF = D_V // 2
TOKENS = 1024
K = HEADS * HALF
N1 = 768
N2 = 256
D_MODEL = N1 + N2
BANK = 512
EPS = 1e-3
TINY = 1e-30
TILES = TOKENS // P

TAIL_TILES = 3
RAMP = 256

FLOPS = 2 * TOKENS * K * D_MODEL


def tile_multiheadattention_pa_kernel(tc, attn_out, inp, w_proj1, w_proj2, ln_a, ln_b, out):
    nc = tc.nc
    attn = attn_out.rearrange("h b l d -> h (b l) d")

    with ExitStack() as ctx:
        keep = ctx.enter_context(tc.tile_pool(name="keep", bufs=1))
        splits = ctx.enter_context(tc.tile_pool(name="splits", bufs=4))
        stage = ctx.enter_context(tc.tile_pool(name="stage", bufs=3))
        work = ctx.enter_context(tc.tile_pool(name="work", bufs=TILES))
        small = ctx.enter_context(tc.tile_pool(name="small", bufs=TILES))
        row_psum = ctx.enter_context(tc.psum_pool(name="row_psum", bufs=1))
        y_psum = ctx.enter_context(tc.psum_pool(name="y_psum", bufs=2))
        t_psum = ctx.enter_context(tc.psum_pool(name="t_psum", bufs=2))
        ctx.enter_context(tc.manual_schedule())

        rows = keep.tile([P, 2 * D_MODEL], BF16)
        nc.vector.memset(rows[:], 0.0)
        ones = keep.tile([P, P], BF16)
        nc.vector.memset(ones[:], 1.0)
        one = keep.tile([P, 1], F32)
        nc.vector.memset(one[:], 1.0)
        warm = keep.tile([P, 1], F32)
        nc.scalar.activation(out=warm[:], in_=one[:], func=ACT.Sqrt)
        ident = keep.tile([P, P], F32)
        make_identity(nc, ident[:])

        x_raw = {}
        x_split = {}
        inp_sb = {}
        out_rows = {}

        def group(first, width):
            tokens = slice(first * P, (first + width) * P)
            for j in range(width):
                out_rows[first + j] = out[tokens, :].rearrange("(p j) n -> p j n", j=width)[:, j, :]
            return tokens

        def load_attention(first, width):
            tokens = group(first, width)
            x_g = keep.tile([P, HEADS, width, D_V], BF16, name="x_raw%d" % first)
            nc.sync.dma_start(
                out=x_g[:].rearrange("p h j d -> p h (j d)"),
                in_=attn[:, tokens, :].rearrange("h (p j) d -> p h (j d)", j=width),
            )
            for j in range(width):
                x_raw[first + j] = x_g[:, :, j, :]

        def load_sorted_attention(k):
            tokens = group(k, 1)
            split = keep.tile([P, 2, K], BF16, name="x_sorted%d" % k)
            for s in range(2):
                nc.sync.dma_start(
                    out=split[:, s, :].rearrange("p (h j) -> p h j", j=HALF),
                    in_=attn[:, tokens, s * HALF : (s + 1) * HALF].rearrange("h p j -> p h j"),
                )
            x_split[k] = split

        def load_residual(first, width):
            tokens = slice(first * P, (first + width) * P)
            inp_g = keep.tile([P, width, D_MODEL], BF16, name="inp%d" % first)
            nc.sync.dma_start(out=inp_g[:], in_=inp[tokens, :].rearrange("(p j) n -> p j n", j=width))
            for j in range(width):
                inp_sb[first + j] = inp_g[:, j, :]

        load_attention(0, 1)
        w1_rows = w_proj1.rearrange("(q t) n -> q t n", t=4)
        w1_low = keep.tile([P, 4, BANK], BF16)
        nc.sync.dma_start(out=w1_low[:], in_=w1_rows[:, :, 0:BANK])
        nc.sync.dma_start(out=rows[0:1, 0:D_MODEL], in_=ln_a.unsqueeze(0))
        nc.sync.dma_start(out=rows[0:1, D_MODEL : 2 * D_MODEL], in_=ln_b.unsqueeze(0))
        w1_high = keep.tile([P, 4, N1 - BANK], BF16)
        nc.sync.dma_start(out=w1_high[:], in_=w1_rows[:, :, BANK:N1])
        w2_raw = keep.tile([P, 4, N2], BF16)
        nc.sync.dma_start(out=w2_raw[:], in_=w_proj2.rearrange("(q t) n -> q t n", t=4))
        load_attention(1, 1)
        load_residual(0, 1)
        load_attention(2, 2)
        load_residual(1, 1)
        load_attention(4, 1)
        load_residual(2, 2)
        load_sorted_attention(5)
        load_residual(4, 1)
        load_sorted_attention(6)
        load_residual(5, 1)
        load_sorted_attention(7)
        load_residual(6, 1)
        load_residual(7, 1)

        w_grouped = keep.tile([P, D_MODEL, 4], BF16, align_bytes=64)
        w_codes = keep.tile([P, D_MODEL], U32, align_bytes=64)
        w_scales = keep.tile([P, D_MODEL], U8, align_bytes=64)

        def regroup_weight(copy, first, raw_cols):
            width = raw_cols.shape[2]
            copy(
                out=w_grouped[:, first : first + width, :].rearrange("p (c i) t -> p c t i", i=4),
                in_=raw_cols.rearrange("p t (c i) -> p c t i", i=4),
            )

        def quantise_weight(c):
            cols = slice(c * BANK, (c + 1) * BANK)
            nc.vector.quantize_mx(
                out=w_codes[:, cols].bitcast(FP8X4),
                scales=w_scales[:, cols],
                in_=w_grouped[:, cols, :].rearrange("p n t -> p (n t)"),
            )

        o_codes = keep.tile([P, TILES, 2 * P], U32, align_bytes=64)
        o_scales = keep.tile([P, TILES, 2 * P], U8, align_bytes=64)
        xt = {}
        grouped = {}
        y = {}
        z = {}
        sums = {}
        neg_mean = {}
        sum_sq = {}
        sigma = {}
        gained = {}
        denom = {}
        inv = {}
        result = {}

        def sort_features(k):
            split = splits.tile([P, 2, K], BF16, name="x_split")
            nc.vector.tensor_copy(
                out=split[:].rearrange("p s (h j) -> p s h j", j=HALF),
                in_=x_raw[k].rearrange("p h (s j) -> p s h j", s=2),
            )
            x_split[k] = split

        def flip(k):
            words = x_split[k][:].bitcast(F32)
            planes = t_psum.tile([P, 2, 2, P], F32, name="xt")
            for s in range(2):
                for u in range(2):
                    nc.tensor.transpose(planes[:, s, u, :], words[:, s, u : 2 * P : 2], ident[:])
            xt[k] = planes

        def evacuate(k):
            packed = stage.tile([P, 2, P, 4], BF16, align_bytes=64, name="grouped")
            nc.scalar.copy(out=packed[:].bitcast(F32), in_=xt[k][:].rearrange("p s u m -> p s m u"))
            grouped[k] = packed

        def quantise(k):
            nc.vector.quantize_mx(
                out=o_codes[:, k, :].bitcast(FP8X4),
                scales=o_scales[:, k, :],
                in_=grouped[k][:].rearrange("p s m t -> p (s m t)"),
            )

        def project(k, c):
            def mx(acc, s, cols):
                nc.tensor.matmul_mx(
                    out=acc,
                    lhsT=o_codes[:, k, s * P : (s + 1) * P].bitcast(FP8X4),
                    lhsT_scale=o_scales[:, k, s * P : (s + 1) * P],
                    rhs=w_codes[:, cols].bitcast(FP8X4),
                    rhs_scale=w_scales[:, cols],
                    start=True,
                    stop=True,
                )

            bank = y_psum.tile([P, BANK], F32, name="y%d" % c)
            if c == 0:
                mx(bank[:], 0, slice(0, BANK))
            else:
                mx(bank[:, 0 : N1 - BANK], 0, slice(BANK, N1))
                mx(bank[:, N1 - BANK : BANK], 1, slice(N1, D_MODEL))
            y[k, c] = bank

        def add_residual(k):
            z_k = work.tile([P, D_MODEL], F32, name="z")
            sums_k = small.tile([P, 2], F32, name="sums")
            for c in range(2):
                cols = slice(c * BANK, (c + 1) * BANK)
                nc.vector.scalar_tensor_tensor(
                    out=z_k[:, cols], in0=inp_sb[k][:, cols], scalar=1.0, in1=y[k, c][:],
                    op0=ALU.mult, op1=ALU.add, accum_out=sums_k[:, c : c + 1],
                )
            z[k] = z_k
            sums[k] = sums_k

        def mean(k):
            neg = small.tile([P, 1], F32, name="neg_mean")
            nc.vector.tensor_scalar(
                out=neg[:], in0=sums[k][:, 0:1], scalar1=sums[k][:, 1:2], scalar2=-1.0 / D_MODEL, op0=ALU.add, op1=ALU.mult
            )
            neg_mean[k] = neg

        def squares(k):
            unused = work.tile([P, D_MODEL], BF16, name="squares")
            total = small.tile([P, 1], F32, name="sum_sq")
            nc.scalar.activation(out=unused[:], in_=z[k][:], func=ACT.Square, bias=neg_mean[k][:], scale=1.0, accum_out=total[:])
            sum_sq[k] = total

        def root(k):
            sigma_k = small.tile([P, 1], F32, name="sigma")
            nc.scalar.activation(out=sigma_k[:], in_=sum_sq[k][:], func=ACT.Sqrt, bias=TINY, scale=1.0 / (D_MODEL - 1))
            sigma[k] = sigma_k

        def apply_gain(k):
            gained_k = work.tile([P, D_MODEL], F32, name="gained")
            nc.vector.scalar_tensor_tensor(
                out=gained_k[:], in0=z[k][:], scalar=neg_mean[k][:], in1=gain[:], op0=ALU.add, op1=ALU.mult
            )
            gained[k] = gained_k

        def add_eps(k):
            denom_k = small.tile([P, 1], F32, name="denom")
            nc.vector.tensor_scalar_add(out=denom_k[:], in0=sigma[k][:], scalar1=EPS)
            denom[k] = denom_k

        def invert(k):
            inv_k = small.tile([P, 1], F32, name="inv")
            nc.vector.reciprocal(out=inv_k[:], in_=denom[k][:])
            inv[k] = inv_k

        def store(k, low, high):
            nc.sync.dma_start(out=out_rows[k][:, low:high], in_=result[k][:, low:high])

        def finish(k):
            v_cols = max(0, RAMP * (k + 1 - (TILES - TAIL_TILES)))
            result_k = work.tile([P, D_MODEL], F32, name="result")
            result[k] = result_k
            if v_cols > 0:
                nc.vector.scalar_tensor_tensor(
                    out=result_k[:, :v_cols], in0=gained[k][:, :v_cols], scalar=inv[k][:], in1=bias_psum[:, :v_cols],
                    op0=ALU.mult, op1=ALU.add,
                )
                store(k, 0, v_cols)
            scaled = work.tile([P, D_MODEL], F32)
            nc.scalar.activation(out=scaled[:, v_cols:], in_=gained[k][:, v_cols:], func=ACT.Copy, scale=inv[k][:])
            nc.gpsimd.tensor_tensor(out=result_k[:, v_cols:], in0=scaled[:, v_cols:], in1=bias[:, v_cols:], op=ALU.add)
            store(k, v_cols, D_MODEL)

        sort_features(0)
        flip(0)
        evacuate(0)

        def repeat_row(first, spread):
            for c in range(2):
                cols = slice(c * BANK, (c + 1) * BANK)
                nc.tensor.matmul(
                    out=spread[:, cols], lhsT=ones[:], rhs=rows[:, first + c * BANK : first + (c + 1) * BANK], start=True, stop=True
                )

        gain = row_psum.tile([P, D_MODEL], BF16)
        repeat_row(0, gain)
        bias_psum = row_psum.tile([P, D_MODEL], BF16)
        repeat_row(D_MODEL, bias_psum)
        regroup_weight(nc.vector.tensor_copy, 0, w1_low[:])
        regroup_weight(nc.scalar.copy, BANK, w1_high[:])
        quantise(0)
        quantise_weight(0)
        project(0, 0)
        regroup_weight(nc.vector.tensor_copy, N1, w2_raw[:])
        sort_features(1)
        flip(1)
        quantise_weight(1)
        project(0, 1)
        bias = keep.tile([P, D_MODEL], BF16)
        nc.scalar.copy(out=bias[:], in_=bias_psum[:])
        evacuate(1)

        def at(k, stage_of, *args):
            if 0 <= k < TILES:
                stage_of(k, *args)

        for k in range(TILES + 1):
            at(k, add_residual)
            if k == TILES:
                apply_gain(k - 1)
            at(k - 1, add_eps)
            at(k + 1, quantise)
            at(k + 1, project, 0)
            at(k + 1, project, 1)
            at(k, mean)
            at(k, squares)
            if k == 0:
                for t in (2, 3):
                    sort_features(t)
                    flip(t)
            at(k + 2, evacuate)
            if 4 <= k + 4 < 5:
                sort_features(k + 4)
            at(k + 4, flip)
            at(k - 1, invert)
            if k < TILES:
                at(k - 1, apply_gain)
            at(k, root)
            at(k - 1, finish)
